import numpy as np
import ml_dtypes

BF16 = ml_dtypes.bfloat16


def bf(x):
    return np.asarray(x, np.float32).astype(BF16)


def f32(x):
    return np.asarray(x, np.float32)


def f64(x):
    return np.asarray(x).astype(np.float64)


def striped(idx):
    return np.tile(idx.reshape(-1, 16).T, (8, 1))


D_IN, D, K, C, S, N = 256, 128, 8, 1024, 512, 1024


def setup_inputs():
    return {
        "cw": f32(0.25 * np.random.standard_normal((C, S))),
        "x": bf(np.random.standard_normal((D_IN, N))),
        "ws": bf(np.random.standard_normal((D_IN, D)) / np.sqrt(D_IN)),
        "bs": f32(0.1 * np.random.standard_normal((D, 1))),
        "offs": striped(np.random.permutation(np.tile(np.arange(S), 2))[:N]),
    }


def reference(cw, x, ws, bs, offs):
    idx = offs[:16].T.reshape(-1)
    e = f64(ws).T @ f64(x) + f64(bs)
    picked = f64(cw)[:, idx].reshape(K, D, N)
    return (picked * e[None, :, :]).sum(axis=1)

@@ -1,0 +1,89 @@
+import concourse.mybir as mybir
+
+F32 = mybir.dt.float32
+BF16 = mybir.dt.bfloat16
+U16 = mybir.dt.uint16
+MULT = mybir.AluOpType.mult
+IDENTITY = mybir.ActivationFunctionType.Identity
+
+P = 128
+D_IN = 256
+CHUNKS = D_IN // P
+CHILDREN = 8
+PARENTS = 512
+SAMPLES = 1024
+PIECE = 512
+PIECES = SAMPLES // PIECE
+PIECE_OFFSET_COLUMNS = PIECE // 16
+
+FLOPS = 2 * D_IN * P * SAMPLES + 2 * CHILDREN * P * SAMPLES
+
+
+def tile_jointembeddingclassifier_kernel(tc, cw, x, ws, bs, offs, out):
+    nc = tc.nc
+    with (
+        tc.tile_pool(name="held", bufs=1) as held,
+        tc.tile_pool(name="products", bufs=4) as products,
+        tc.tile_pool(name="rounded", bufs=4) as rounded_pool,
+        tc.tile_pool(name="staging", bufs=2) as staging,
+        tc.psum_pool(name="psum", bufs=1) as psum,
+    ):
+        offsets = held.tile([P, SAMPLES // 16], U16, name="offsets")
+        nc.sync.dma_start(offsets[:], offs)
+
+        bias = held.tile([P, 1], F32, name="bias")
+        nc.gpsimd.dma_start(bias[:], bs)
+
+        queues = [nc.sync, nc.scalar]
+        ws_chunks = [held.tile([P, P], BF16, name=f"ws{c}") for c in range(CHUNKS)]
+        x_chunks = [held.tile([P, SAMPLES], BF16, name=f"x{c}") for c in range(CHUNKS)]
+        for c in range(CHUNKS):
+            queues[c % 2].dma_start(ws_chunks[c][:], ws[c * P : (c + 1) * P, :])
+            queues[c % 2].dma_start(x_chunks[c][:, 0:PIECE], x[c * P : (c + 1) * P, 0:PIECE])
+
+        blocks = [held.tile([P, PARENTS], F32, name=f"block{k}") for k in range(CHILDREN)]
+        for k in range(CHILDREN):
+            queues[k % 2].dma_start(blocks[k][:], cw[k * P : (k + 1) * P, :])
+
+        for c in range(CHUNKS):
+            queues[c % 2].dma_start(x_chunks[c][:, PIECE:SAMPLES], x[c * P : (c + 1) * P, PIECE:SAMPLES])
+
+        selector = held.tile([P, 2 * CHILDREN - 1], BF16, name="selector")
+        nc.gpsimd.memset(selector[:], 0.0)
+        nc.gpsimd.memset(selector[:, CHILDREN - 1 : CHILDREN], 1.0)
+
+        e_pieces = []
+        for h in range(PIECES):
+            e_psum = psum.tile([P, PIECE], F32, name=f"e_psum{h}")
+            for c in range(CHUNKS):
+                nc.tensor.matmul(
+                    e_psum[:],
+                    ws_chunks[c][:],
+                    x_chunks[c][:, h * PIECE : (h + 1) * PIECE],
+                    start=(c == 0),
+                    stop=(c == CHUNKS - 1),
+                )
+            e_piece = held.tile([P, PIECE], F32, name=f"e{h}")
+            nc.scalar.activation(e_piece[:], e_psum[:], IDENTITY, bias=bias[:])
+            e_pieces.append(e_piece)
+
+        for h in range(PIECES):
+            piece_offsets = offsets[:, h * PIECE_OFFSET_COLUMNS : (h + 1) * PIECE_OFFSET_COLUMNS]
+            logits = psum.tile([CHILDREN, PIECE], F32, name=f"logits{h}")
+            for k in range(CHILDREN):
+                product = products.tile([P, PIECE], F32, name="product")
+                nc.vector.tensor_tensor(
+                    product[:], blocks[k][:].indirect(piece_offsets), e_pieces[h][:], MULT
+                )
+                rounded = rounded_pool.tile([P, PIECE], BF16, name="rounded")
+                nc.scalar.copy(rounded[:], product[:])
+                nc.tensor.matmul(
+                    logits[:],
+                    selector[:, CHILDREN - 1 - k : 2 * CHILDREN - 1 - k],
+                    rounded[:],
+                    start=(k == 0),
+                    stop=(k == CHILDREN - 1),
+                )
+            staged = staging.tile([CHILDREN, PIECE], F32, name="staged")
+            nc.scalar.copy(staged[:], logits[:])
+            nc.sync.dma_start(out[:, h * PIECE : (h + 1) * PIECE], staged[:])

@@ -32,7 +32,7 @@ def tile_jointembeddingclassifier_kernel(tc, cw, x, ws, bs, offs, out):
         nc.sync.dma_start(offsets[:], offs)
 
         bias = held.tile([P, 1], F32, name="bias")
-        nc.gpsimd.dma_start(bias[:], bs)
+        nc.scalar.dma_start(bias[:], bs)
 
         queues = [nc.sync, nc.scalar]
         ws_chunks = [held.tile([P, P], BF16, name=f"ws{c}") for c in range(CHUNKS)]
@@ -64,7 +64,10 @@ def tile_jointembeddingclassifier_kernel(tc, cw, x, ws, bs, offs, out):
                     stop=(c == CHUNKS - 1),
                 )
             e_piece = held.tile([P, PIECE], F32, name=f"e{h}")
-            nc.scalar.activation(e_piece[:], e_psum[:], IDENTITY, bias=bias[:])
+            if h == 0:
+                nc.vector.tensor_scalar_add(e_piece[:], e_psum[:], bias[:])
+            else:
+                nc.scalar.activation(e_piece[:], e_psum[:], IDENTITY, bias=bias[:])
             e_pieces.append(e_piece)
 
         for h in range(PIECES):

@@ -12,9 +12,13 @@ CHUNKS = D_IN // P
 CHILDREN = 8
 PARENTS = 512
 SAMPLES = 1024
-PIECE = 512
-PIECES = SAMPLES // PIECE
-PIECE_OFFSET_COLUMNS = PIECE // 16
+LIST_COLUMN = 16
+
+PIECE_SIZES = (512, 384, 128)
+PIECE_STARTS = tuple(sum(PIECE_SIZES[:i]) for i in range(len(PIECE_SIZES)))
+assert sum(PIECE_SIZES) == SAMPLES
+assert max(PIECE_SIZES) <= PARENTS
+assert all(start % (2 * LIST_COLUMN) == 0 for start in PIECE_STARTS)
 
 FLOPS = 2 * D_IN * P * SAMPLES + 2 * CHILDREN * P * SAMPLES
 
@@ -26,59 +30,59 @@ def tile_jointembeddingclassifier_kernel(tc, cw, x, ws, bs, offs, out):
         tc.tile_pool(name="products", bufs=4) as products,
         tc.tile_pool(name="rounded", bufs=4) as rounded_pool,
         tc.tile_pool(name="staging", bufs=2) as staging,
-        tc.psum_pool(name="psum", bufs=1) as psum,
+        tc.psum_pool(name="e_banks", bufs=2) as e_banks,
+        tc.psum_pool(name="logit_banks", bufs=2) as logit_banks,
     ):
-        offsets = held.tile([P, SAMPLES // 16], U16, name="offsets")
+        offsets = held.tile([P, SAMPLES // LIST_COLUMN], U16, name="offsets")
         nc.sync.dma_start(offsets[:], offs)
 
         bias = held.tile([P, 1], F32, name="bias")
         nc.scalar.dma_start(bias[:], bs)
 
         queues = [nc.sync, nc.scalar]
+        first_size = PIECE_SIZES[0]
         ws_chunks = [held.tile([P, P], BF16, name=f"ws{c}") for c in range(CHUNKS)]
         x_chunks = [held.tile([P, SAMPLES], BF16, name=f"x{c}") for c in range(CHUNKS)]
         for c in range(CHUNKS):
             queues[c % 2].dma_start(ws_chunks[c][:], ws[c * P : (c + 1) * P, :])
-            queues[c % 2].dma_start(x_chunks[c][:, 0:PIECE], x[c * P : (c + 1) * P, 0:PIECE])
-
+            queues[c % 2].dma_start(x_chunks[c][:, 0:first_size], x[c * P : (c + 1) * P, 0:first_size])
         blocks = [held.tile([P, PARENTS], F32, name=f"block{k}") for k in range(CHILDREN)]
         for k in range(CHILDREN):
             queues[k % 2].dma_start(blocks[k][:], cw[k * P : (k + 1) * P, :])
 
         for c in range(CHUNKS):
-            queues[c % 2].dma_start(x_chunks[c][:, PIECE:SAMPLES], x[c * P : (c + 1) * P, PIECE:SAMPLES])
-
+            queues[c % 2].dma_start(x_chunks[c][:, first_size:SAMPLES], x[c * P : (c + 1) * P, first_size:SAMPLES])
         selector = held.tile([P, 2 * CHILDREN - 1], BF16, name="selector")
         nc.gpsimd.memset(selector[:], 0.0)
         nc.gpsimd.memset(selector[:, CHILDREN - 1 : CHILDREN], 1.0)
 
         e_pieces = []
-        for h in range(PIECES):
-            e_psum = psum.tile([P, PIECE], F32, name=f"e_psum{h}")
+        for i, (start, size) in enumerate(zip(PIECE_STARTS, PIECE_SIZES)):
+            e_psum = e_banks.tile([P, size], F32, name="e_psum")
             for c in range(CHUNKS):
                 nc.tensor.matmul(
                     e_psum[:],
                     ws_chunks[c][:],
-                    x_chunks[c][:, h * PIECE : (h + 1) * PIECE],
+                    x_chunks[c][:, start : start + size],
                     start=(c == 0),
                     stop=(c == CHUNKS - 1),
                 )
-            e_piece = held.tile([P, PIECE], F32, name=f"e{h}")
-            if h == 0:
+            e_piece = held.tile([P, size], F32, name=f"e{i}")
+            if i == 0:
                 nc.vector.tensor_scalar_add(e_piece[:], e_psum[:], bias[:])
             else:
                 nc.scalar.activation(e_piece[:], e_psum[:], IDENTITY, bias=bias[:])
             e_pieces.append(e_piece)
 
-        for h in range(PIECES):
-            piece_offsets = offsets[:, h * PIECE_OFFSET_COLUMNS : (h + 1) * PIECE_OFFSET_COLUMNS]
-            logits = psum.tile([CHILDREN, PIECE], F32, name=f"logits{h}")
+        for e_piece, start, size in zip(e_pieces, PIECE_STARTS, PIECE_SIZES):
+            piece_offsets = offsets[:, start // LIST_COLUMN : (start + size) // LIST_COLUMN]
+            logits = logit_banks.tile([CHILDREN, size], F32, name="logits")
             for k in range(CHILDREN):
-                product = products.tile([P, PIECE], F32, name="product")
+                product = products.tile([P, size], F32, name="product")
                 nc.vector.tensor_tensor(
-                    product[:], blocks[k][:].indirect(piece_offsets), e_pieces[h][:], MULT
+                    product[:], blocks[k][:].indirect(piece_offsets), e_piece[:], MULT
                 )
-                rounded = rounded_pool.tile([P, PIECE], BF16, name="rounded")
+                rounded = rounded_pool.tile([P, size], BF16, name="rounded")
                 nc.scalar.copy(rounded[:], product[:])
                 nc.tensor.matmul(
                     logits[:],
@@ -87,6 +91,6 @@ def tile_jointembeddingclassifier_kernel(tc, cw, x, ws, bs, offs, out):
                     start=(k == 0),
                     stop=(k == CHILDREN - 1),
                 )
-            staged = staging.tile([CHILDREN, PIECE], F32, name="staged")
+            staged = staging.tile([CHILDREN, size], F32, name="staged")
             nc.scalar.copy(staged[:], logits[:])
-            nc.sync.dma_start(out[:, h * PIECE : (h + 1) * PIECE], staged[:])
+            nc.sync.dma_start(out[:, start : start + size], staged[:])

@@ -14,7 +14,7 @@ PARENTS = 512
 SAMPLES = 1024
 LIST_COLUMN = 16
 
-PIECE_SIZES = (512, 384, 128)
+PIECE_SIZES = (512, 448, 64)
 PIECE_STARTS = tuple(sum(PIECE_SIZES[:i]) for i in range(len(PIECE_SIZES)))
 assert sum(PIECE_SIZES) == SAMPLES
 assert max(PIECE_SIZES) <= PARENTS

@@ -14,7 +14,7 @@ PARENTS = 512
 SAMPLES = 1024
 LIST_COLUMN = 16
 
-PIECE_SIZES = (512, 448, 64)
+PIECE_SIZES = (512, 384, 128)
 PIECE_STARTS = tuple(sum(PIECE_SIZES[:i]) for i in range(len(PIECE_SIZES)))
 assert sum(PIECE_SIZES) == SAMPLES
 assert max(PIECE_SIZES) <= PARENTS
@@ -33,12 +33,6 @@ def tile_jointembeddingclassifier_kernel(tc, cw, x, ws, bs, offs, out):
         tc.psum_pool(name="e_banks", bufs=2) as e_banks,
         tc.psum_pool(name="logit_banks", bufs=2) as logit_banks,
     ):
-        offsets = held.tile([P, SAMPLES // LIST_COLUMN], U16, name="offsets")
-        nc.sync.dma_start(offsets[:], offs)
-
-        bias = held.tile([P, 1], F32, name="bias")
-        nc.scalar.dma_start(bias[:], bs)
-
         queues = [nc.sync, nc.scalar]
         first_size = PIECE_SIZES[0]
         ws_chunks = [held.tile([P, P], BF16, name=f"ws{c}") for c in range(CHUNKS)]
@@ -46,6 +40,12 @@ def tile_jointembeddingclassifier_kernel(tc, cw, x, ws, bs, offs, out):
         for c in range(CHUNKS):
             queues[c % 2].dma_start(ws_chunks[c][:], ws[c * P : (c + 1) * P, :])
             queues[c % 2].dma_start(x_chunks[c][:, 0:first_size], x[c * P : (c + 1) * P, 0:first_size])
+
+        bias = held.tile([P, 1], F32, name="bias")
+        nc.scalar.dma_start(bias[:], bs)
+
+        offsets = held.tile([P, SAMPLES // LIST_COLUMN], U16, name="offsets")
+        nc.sync.dma_start(offsets[:], offs)
         blocks = [held.tile([P, PARENTS], F32, name=f"block{k}") for k in range(CHILDREN)]
         for k in range(CHILDREN):
             queues[k % 2].dma_start(blocks[k][:], cw[k * P : (k + 1) * P, :])
@@ -93,4 +93,4 @@ def tile_jointembeddingclassifier_kernel(tc, cw, x, ws, bs, offs, out):
                 )
             staged = staging.tile([CHILDREN, size], F32, name="staged")
             nc.scalar.copy(staged[:], logits[:])
-            nc.sync.dma_start(out[:, start : start + size], staged[:])
+            nc.scalar.dma_start(out[:, start : start + size], staged[:])

@@ -30,9 +30,16 @@ def tile_jointembeddingclassifier_kernel(tc, cw, x, ws, bs, offs, out):
         tc.tile_pool(name="products", bufs=4) as products,
         tc.tile_pool(name="rounded", bufs=4) as rounded_pool,
         tc.tile_pool(name="staging", bufs=2) as staging,
+        tc.psum_pool(name="bias_bank", bufs=1) as bias_bank,
         tc.psum_pool(name="e_banks", bufs=2) as e_banks,
         tc.psum_pool(name="logit_banks", bufs=2) as logit_banks,
     ):
+        offsets = held.tile([P, SAMPLES // LIST_COLUMN], U16, name="offsets")
+        nc.sync.dma_start(offsets[:], offs)
+
+        bias_row = held.tile([1, P], F32, name="bias_row")
+        nc.scalar.dma_start(bias_row[:], bs.rearrange("d one -> one d"))
+
         queues = [nc.sync, nc.scalar]
         first_size = PIECE_SIZES[0]
         ws_chunks = [held.tile([P, P], BF16, name=f"ws{c}") for c in range(CHUNKS)]
@@ -40,12 +47,6 @@ def tile_jointembeddingclassifier_kernel(tc, cw, x, ws, bs, offs, out):
         for c in range(CHUNKS):
             queues[c % 2].dma_start(ws_chunks[c][:], ws[c * P : (c + 1) * P, :])
             queues[c % 2].dma_start(x_chunks[c][:, 0:first_size], x[c * P : (c + 1) * P, 0:first_size])
-
-        bias = held.tile([P, 1], F32, name="bias")
-        nc.scalar.dma_start(bias[:], bs)
-
-        offsets = held.tile([P, SAMPLES // LIST_COLUMN], U16, name="offsets")
-        nc.sync.dma_start(offsets[:], offs)
         blocks = [held.tile([P, PARENTS], F32, name=f"block{k}") for k in range(CHILDREN)]
         for k in range(CHILDREN):
             queues[k % 2].dma_start(blocks[k][:], cw[k * P : (k + 1) * P, :])
@@ -55,6 +56,13 @@ def tile_jointembeddingclassifier_kernel(tc, cw, x, ws, bs, offs, out):
         selector = held.tile([P, 2 * CHILDREN - 1], BF16, name="selector")
         nc.gpsimd.memset(selector[:], 0.0)
         nc.gpsimd.memset(selector[:, CHILDREN - 1 : CHILDREN], 1.0)
+
+        one = held.tile([1, 1], F32, name="one")
+        nc.gpsimd.memset(one[:], 1.0)
+        bias_psum = bias_bank.tile([P, 1], F32, name="bias_psum")
+        nc.tensor.matmul(bias_psum[:], bias_row[:], one[:], start=True, stop=True)
+        bias = held.tile([P, 1], F32, name="bias")
+        nc.vector.tensor_copy(bias[:], bias_psum[:])
 
         e_pieces = []
         for i, (start, size) in enumerate(zip(PIECE_STARTS, PIECE_SIZES)):
@@ -93,4 +101,4 @@ def tile_jointembeddingclassifier_kernel(tc, cw, x, ws, bs, offs, out):
                 )
             staged = staging.tile([CHILDREN, size], F32, name="staged")
             nc.scalar.copy(staged[:], logits[:])
-            nc.scalar.dma_start(out[:, start : start + size], staged[:])
+            nc.sync.dma_start(out[:, start : start + size], staged[:])

@@ -14,11 +14,13 @@ PARENTS = 512
 SAMPLES = 1024
 LIST_COLUMN = 16
 
-PIECE_SIZES = (512, 384, 128)
-PIECE_STARTS = tuple(sum(PIECE_SIZES[:i]) for i in range(len(PIECE_SIZES)))
-assert sum(PIECE_SIZES) == SAMPLES
-assert max(PIECE_SIZES) <= PARENTS
-assert all(start % (2 * LIST_COLUMN) == 0 for start in PIECE_STARTS)
+HALF = PARENTS
+WHOLE = ((0, HALF),)
+HEAD = ((0, HALF // 2), (HALF // 2, HALF // 2))
+EARLY = 2
+SHORT = 128
+TAIL = ((0, HALF - SHORT), (HALF - SHORT, SHORT))
+assert all(start % (2 * LIST_COLUMN) == 0 for start, size in HEAD + TAIL)
 
 FLOPS = 2 * D_IN * P * SAMPLES + 2 * CHILDREN * P * SAMPLES
 
@@ -30,75 +32,107 @@ def tile_jointembeddingclassifier_kernel(tc, cw, x, ws, bs, offs, out):
         tc.tile_pool(name="products", bufs=4) as products,
         tc.tile_pool(name="rounded", bufs=4) as rounded_pool,
         tc.tile_pool(name="staging", bufs=2) as staging,
-        tc.psum_pool(name="bias_bank", bufs=1) as bias_bank,
-        tc.psum_pool(name="e_banks", bufs=2) as e_banks,
-        tc.psum_pool(name="logit_banks", bufs=2) as logit_banks,
+        tc.psum_pool(name="e_banks", bufs=3) as e_banks,
+        tc.psum_pool(name="logit_banks", bufs=1) as logit_banks,
     ):
-        offsets = held.tile([P, SAMPLES // LIST_COLUMN], U16, name="offsets")
-        nc.sync.dma_start(offsets[:], offs)
-
-        bias_row = held.tile([1, P], F32, name="bias_row")
-        nc.scalar.dma_start(bias_row[:], bs.rearrange("d one -> one d"))
-
-        queues = [nc.sync, nc.scalar]
-        first_size = PIECE_SIZES[0]
-        ws_chunks = [held.tile([P, P], BF16, name=f"ws{c}") for c in range(CHUNKS)]
-        x_chunks = [held.tile([P, SAMPLES], BF16, name=f"x{c}") for c in range(CHUNKS)]
-        for c in range(CHUNKS):
-            queues[c % 2].dma_start(ws_chunks[c][:], ws[c * P : (c + 1) * P, :])
-            queues[c % 2].dma_start(x_chunks[c][:, 0:first_size], x[c * P : (c + 1) * P, 0:first_size])
+        ws_chunks = held.tile([P, CHUNKS, P], BF16, name="ws_chunks")
+        x_chunks = held.tile([P, CHUNKS, SAMPLES], BF16, name="x_chunks")
+        x_by_chunk = x.rearrange("(c p) j -> p c j", p=P)
         blocks = [held.tile([P, PARENTS], F32, name=f"block{k}") for k in range(CHILDREN)]
-        for k in range(CHILDREN):
-            queues[k % 2].dma_start(blocks[k][:], cw[k * P : (k + 1) * P, :])
+        bias = held.tile([P, 1], F32, name="bias")
+        offsets = held.tile([P, SAMPLES // LIST_COLUMN], U16, name="offsets")
 
-        for c in range(CHUNKS):
-            queues[c % 2].dma_start(x_chunks[c][:, first_size:SAMPLES], x[c * P : (c + 1) * P, first_size:SAMPLES])
+        def load_x(start, size):
+            nc.sync.dma_start(x_chunks[:, :, start : start + size], x_by_chunk[:, :, start : start + size])
+
+        def load_block(queue, k):
+            queue.dma_start(blocks[k][:], cw[k * P : (k + 1) * P, :])
+
+        nc.scalar.dma_start(ws_chunks[:], ws.rearrange("(c p) d -> p c d", p=P))
+        load_block(nc.scalar, 0)
+        load_x(*HEAD[0])
+        nc.sync.dma_start(bias[:], bs)
+        nc.sync.dma_start(offsets[:], offs)
+        load_x(*HEAD[1])
+        for k in range(1, CHILDREN):
+            load_block(nc.sync, k)
+        load_x(HALF, HALF)
+
         selector = held.tile([P, 2 * CHILDREN - 1], BF16, name="selector")
         nc.gpsimd.memset(selector[:], 0.0)
         nc.gpsimd.memset(selector[:, CHILDREN - 1 : CHILDREN], 1.0)
 
-        one = held.tile([1, 1], F32, name="one")
-        nc.gpsimd.memset(one[:], 1.0)
-        bias_psum = bias_bank.tile([P, 1], F32, name="bias_psum")
-        nc.tensor.matmul(bias_psum[:], bias_row[:], one[:], start=True, stop=True)
-        bias = held.tile([P, 1], F32, name="bias")
-        nc.vector.tensor_copy(bias[:], bias_psum[:])
+        e_all = held.tile([P, SAMPLES], F32, name="e_all")
 
-        e_pieces = []
-        for i, (start, size) in enumerate(zip(PIECE_STARTS, PIECE_SIZES)):
+        def project(start, size, add_bias_on_vector):
             e_psum = e_banks.tile([P, size], F32, name="e_psum")
             for c in range(CHUNKS):
                 nc.tensor.matmul(
                     e_psum[:],
-                    ws_chunks[c][:],
-                    x_chunks[c][:, start : start + size],
+                    ws_chunks[:, c, :],
+                    x_chunks[:, c, start : start + size],
                     start=(c == 0),
                     stop=(c == CHUNKS - 1),
                 )
-            e_piece = held.tile([P, size], F32, name=f"e{i}")
-            if i == 0:
-                nc.vector.tensor_scalar_add(e_piece[:], e_psum[:], bias[:])
+            if add_bias_on_vector:
+                nc.vector.tensor_scalar_add(e_all[:, start : start + size], e_psum[:], bias[:])
             else:
-                nc.scalar.activation(e_piece[:], e_psum[:], IDENTITY, bias=bias[:])
-            e_pieces.append(e_piece)
+                nc.scalar.activation(e_all[:, start : start + size], e_psum[:], IDENTITY, bias=bias[:])
 
-        for e_piece, start, size in zip(e_pieces, PIECE_STARTS, PIECE_SIZES):
-            piece_offsets = offsets[:, start // LIST_COLUMN : (start + size) // LIST_COLUMN]
-            logits = logit_banks.tile([CHILDREN, size], F32, name="logits")
-            for k in range(CHILDREN):
-                product = products.tile([P, size], F32, name="product")
-                nc.vector.tensor_tensor(
-                    product[:], blocks[k][:].indirect(piece_offsets), e_piece[:], MULT
-                )
-                rounded = rounded_pool.tile([P, size], BF16, name="rounded")
-                nc.scalar.copy(rounded[:], product[:])
-                nc.tensor.matmul(
-                    logits[:],
-                    selector[:, CHILDREN - 1 - k : 2 * CHILDREN - 1 - k],
-                    rounded[:],
-                    start=(k == 0),
-                    stop=(k == CHILDREN - 1),
-                )
+        project(*HEAD[0], add_bias_on_vector=True)
+        project(*HEAD[1], add_bias_on_vector=False)
+        project(HALF, HALF, add_bias_on_vector=False)
+
+        def look_up(product, rounded, k, half_start, start, size):
+            first_column = (half_start + start) // LIST_COLUMN
+            nc.vector.tensor_tensor(
+                product[:, start : start + size],
+                blocks[k][:].indirect(offsets[:, first_column : first_column + size // LIST_COLUMN]),
+                e_all[:, half_start + start : half_start + start + size],
+                MULT,
+            )
+            nc.scalar.copy(rounded[:, start : start + size], product[:, start : start + size])
+
+        def add_up(logits, rounded, k, start, size):
+            nc.tensor.matmul(
+                logits[:],
+                selector[:, CHILDREN - 1 - k : 2 * CHILDREN - 1 - k],
+                rounded[:, start : start + size],
+                start=(k == 0),
+                stop=(k == CHILDREN - 1),
+            )
+
+        def store(logits, first_sample, size):
             staged = staging.tile([CHILDREN, size], F32, name="staged")
             nc.scalar.copy(staged[:], logits[:])
-            nc.sync.dma_start(out[:, start : start + size], staged[:])
+            nc.sync.dma_start(out[:, first_sample : first_sample + size], staged[:])
+
+        def new_tiles(k):
+            product = products.tile([P, HALF], F32, name=f"product{k}", tag="product")
+            rounded = rounded_pool.tile([P, HALF], BF16, name=f"rounded{k}", tag="rounded")
+            return product, rounded
+
+        logits = logit_banks.tile([CHILDREN, HALF], F32, name="logits_first")
+        early_tiles = [new_tiles(k) for k in range(EARLY)]
+        for start, size in HEAD:
+            for k in range(EARLY):
+                look_up(*early_tiles[k], k, 0, start, size)
+        for k in range(EARLY):
+            add_up(logits, early_tiles[k][1], k, 0, HALF)
+        for k in range(EARLY, CHILDREN):
+            product, rounded = new_tiles(k)
+            look_up(product, rounded, k, 0, 0, HALF)
+            add_up(logits, rounded, k, 0, HALF)
+        store(logits, 0, HALF)
+
+        tail_logits = [
+            logit_banks.tile([CHILDREN, size], F32, name=f"logits_tail{start}") for start, size in TAIL
+        ]
+        for k in range(CHILDREN):
+            product, rounded = new_tiles(k)
+            for start, size in TAIL if k == CHILDREN - 1 else WHOLE:
+                look_up(product, rounded, k, HALF, start, size)
+            for range_logits, (start, size) in zip(tail_logits, TAIL):
+                add_up(range_logits, rounded, k, start, size)
+        for range_logits, (start, size) in zip(tail_logits, TAIL):
+            store(range_logits, HALF + start, size)

@@ -37,7 +37,7 @@ def tile_jointembeddingclassifier_kernel(tc, cw, x, ws, bs, offs, out):
     ):
         ws_chunks = held.tile([P, CHUNKS, P], BF16, name="ws_chunks")
         x_chunks = held.tile([P, CHUNKS, SAMPLES], BF16, name="x_chunks")
-        x_by_chunk = x.rearrange("(c p) j -> p c j", p=P)
+        x_by_chunk = x.rearrange("(p c) j -> p c j", c=CHUNKS)
         blocks = [held.tile([P, PARENTS], F32, name=f"block{k}") for k in range(CHILDREN)]
         bias = held.tile([P, 1], F32, name="bias")
         offsets = held.tile([P, SAMPLES // LIST_COLUMN], U16, name="offsets")
@@ -48,19 +48,24 @@ def tile_jointembeddingclassifier_kernel(tc, cw, x, ws, bs, offs, out):
         def load_block(queue, k):
             queue.dma_start(blocks[k][:], cw[k * P : (k + 1) * P, :])
 
-        nc.scalar.dma_start(ws_chunks[:], ws.rearrange("(c p) d -> p c d", p=P))
+        nc.scalar.dma_start(ws_chunks[:], ws.rearrange("(p c) d -> p c d", c=CHUNKS))
         load_block(nc.scalar, 0)
-        load_x(*HEAD[0])
+        load_x(0, HALF)
         nc.sync.dma_start(bias[:], bs)
         nc.sync.dma_start(offsets[:], offs)
-        load_x(*HEAD[1])
-        for k in range(1, CHILDREN):
-            load_block(nc.sync, k)
+        load_block(nc.sync, 1)
         load_x(HALF, HALF)
+        for k in range(2, CHILDREN):
+            load_block(nc.sync, k)
 
         selector = held.tile([P, 2 * CHILDREN - 1], BF16, name="selector")
         nc.gpsimd.memset(selector[:], 0.0)
         nc.gpsimd.memset(selector[:, CHILDREN - 1 : CHILDREN], 1.0)
+
+        cold = held.tile([P, 1], F32, name="cold")
+        nc.gpsimd.memset(cold[:], 0.0)
+        warm = held.tile([P, 1], F32, name="warm")
+        nc.scalar.copy(warm[:], cold[:])
 
         e_all = held.tile([P, SAMPLES], F32, name="e_all")
 

@@ -15,12 +15,13 @@ SAMPLES = 1024
 LIST_COLUMN = 16
 
 HALF = PARENTS
+PART = HALF // 2
 WHOLE = ((0, HALF),)
-HEAD = ((0, HALF // 2), (HALF // 2, HALF // 2))
-EARLY = 2
+BY_PARTS = ((0, PART), (PART, PART))
 SHORT = 128
 TAIL = ((0, HALF - SHORT), (HALF - SHORT, SHORT))
-assert all(start % (2 * LIST_COLUMN) == 0 for start, size in HEAD + TAIL)
+GROUPS = ((0, 1), (2, 3), (4, 5, 6, 7))
+assert all(start % (2 * LIST_COLUMN) == 0 for start, size in BY_PARTS + TAIL)
 
 FLOPS = 2 * D_IN * P * SAMPLES + 2 * CHILDREN * P * SAMPLES
 
@@ -53,9 +54,8 @@ def tile_jointembeddingclassifier_kernel(tc, cw, x, ws, bs, offs, out):
         load_x(0, HALF)
         nc.sync.dma_start(bias[:], bs)
         nc.sync.dma_start(offsets[:], offs)
-        load_block(nc.sync, 1)
         load_x(HALF, HALF)
-        for k in range(2, CHILDREN):
+        for k in range(1, CHILDREN):
             load_block(nc.sync, k)
 
         selector = held.tile([P, 2 * CHILDREN - 1], BF16, name="selector")
@@ -68,8 +68,7 @@ def tile_jointembeddingclassifier_kernel(tc, cw, x, ws, bs, offs, out):
         nc.scalar.copy(warm[:], cold[:])
 
         e_all = held.tile([P, SAMPLES], F32, name="e_all")
-
-        def project(start, size, add_bias_on_vector):
+        for start, size in BY_PARTS + ((HALF, HALF),):
             e_psum = e_banks.tile([P, size], F32, name="e_psum")
             for c in range(CHUNKS):
                 nc.tensor.matmul(
@@ -79,24 +78,24 @@ def tile_jointembeddingclassifier_kernel(tc, cw, x, ws, bs, offs, out):
                     start=(c == 0),
                     stop=(c == CHUNKS - 1),
                 )
-            if add_bias_on_vector:
+            if start == 0:
                 nc.vector.tensor_scalar_add(e_all[:, start : start + size], e_psum[:], bias[:])
             else:
                 nc.scalar.activation(e_all[:, start : start + size], e_psum[:], IDENTITY, bias=bias[:])
 
-        project(*HEAD[0], add_bias_on_vector=True)
-        project(*HEAD[1], add_bias_on_vector=False)
-        project(HALF, HALF, add_bias_on_vector=False)
-
-        def look_up(product, rounded, k, half_start, start, size):
-            first_column = (half_start + start) // LIST_COLUMN
-            nc.vector.tensor_tensor(
-                product[:, start : start + size],
-                blocks[k][:].indirect(offsets[:, first_column : first_column + size // LIST_COLUMN]),
-                e_all[:, half_start + start : half_start + start + size],
-                MULT,
-            )
-            nc.scalar.copy(rounded[:, start : start + size], product[:, start : start + size])
+        def look_up(k, half_start, cuts):
+            product = products.tile([P, HALF], F32, name="product")
+            rounded = rounded_pool.tile([P, HALF], BF16, name="rounded")
+            for start, size in cuts:
+                first_column = (half_start + start) // LIST_COLUMN
+                nc.vector.tensor_tensor(
+                    product[:, start : start + size],
+                    blocks[k][:].indirect(offsets[:, first_column : first_column + size // LIST_COLUMN]),
+                    e_all[:, half_start + start : half_start + start + size],
+                    MULT,
+                )
+                nc.scalar.copy(rounded[:, start : start + size], product[:, start : start + size])
+            return rounded
 
         def add_up(logits, rounded, k, start, size):
             nc.tensor.matmul(
@@ -112,32 +111,25 @@ def tile_jointembeddingclassifier_kernel(tc, cw, x, ws, bs, offs, out):
             nc.scalar.copy(staged[:], logits[:])
             nc.sync.dma_start(out[:, first_sample : first_sample + size], staged[:])
 
-        def new_tiles(k):
-            product = products.tile([P, HALF], F32, name=f"product{k}", tag="product")
-            rounded = rounded_pool.tile([P, HALF], BF16, name=f"rounded{k}", tag="rounded")
-            return product, rounded
-
-        logits = logit_banks.tile([CHILDREN, HALF], F32, name="logits_first")
-        early_tiles = [new_tiles(k) for k in range(EARLY)]
-        for start, size in HEAD:
-            for k in range(EARLY):
-                look_up(*early_tiles[k], k, 0, start, size)
-        for k in range(EARLY):
-            add_up(logits, early_tiles[k][1], k, 0, HALF)
-        for k in range(EARLY, CHILDREN):
-            product, rounded = new_tiles(k)
-            look_up(product, rounded, k, 0, 0, HALF)
-            add_up(logits, rounded, k, 0, HALF)
-        store(logits, 0, HALF)
-
+        first_logits = logit_banks.tile([CHILDREN, HALF], F32, name="first_logits")
         tail_logits = [
-            logit_banks.tile([CHILDREN, size], F32, name=f"logits_tail{start}") for start, size in TAIL
+            logit_banks.tile([CHILDREN, size], F32, name=f"tail_logits{start}") for start, size in TAIL
         ]
-        for k in range(CHILDREN):
-            product, rounded = new_tiles(k)
-            for start, size in TAIL if k == CHILDREN - 1 else WHOLE:
-                look_up(product, rounded, k, HALF, start, size)
+
+        def first_half(k, cuts):
+            add_up(first_logits, look_up(k, 0, cuts), k, 0, HALF)
+
+        def second_half(k, cuts):
+            rounded = look_up(k, HALF, cuts)
             for range_logits, (start, size) in zip(tail_logits, TAIL):
                 add_up(range_logits, rounded, k, start, size)
+
+        for group in GROUPS:
+            for k in group:
+                first_half(k, BY_PARTS if k == 0 else WHOLE)
+            if group == GROUPS[-1]:
+                store(first_logits, 0, HALF)
+            for k in group:
+                second_half(k, TAIL if k == CHILDREN - 1 else WHOLE)
         for range_logits, (start, size) in zip(tail_logits, TAIL):
             store(range_logits, HALF + start, size)

@@ -50,8 +50,8 @@ def tile_jointembeddingclassifier_kernel(tc, cw, x, ws, bs, offs, out):
             queue.dma_start(blocks[k][:], cw[k * P : (k + 1) * P, :])
 
         nc.scalar.dma_start(ws_chunks[:], ws.rearrange("(p c) d -> p c d", c=CHUNKS))
-        load_block(nc.scalar, 0)
         load_x(0, HALF)
+        load_block(nc.sync, 0)
         nc.sync.dma_start(bias[:], bs)
         nc.sync.dma_start(offsets[:], offs)
         load_x(HALF, HALF)

@@ -18,7 +18,7 @@ HALF = PARENTS
 PART = HALF // 2
 WHOLE = ((0, HALF),)
 BY_PARTS = ((0, PART), (PART, PART))
-SHORT = 128
+SHORT = 256
 TAIL = ((0, HALF - SHORT), (HALF - SHORT, SHORT))
 GROUPS = ((0, 1), (2, 3), (4, 5, 6, 7))
 assert all(start % (2 * LIST_COLUMN) == 0 for start, size in BY_PARTS + TAIL)
@@ -83,7 +83,7 @@ def tile_jointembeddingclassifier_kernel(tc, cw, x, ws, bs, offs, out):
             else:
                 nc.scalar.activation(e_all[:, start : start + size], e_psum[:], IDENTITY, bias=bias[:])
 
-        def look_up(k, half_start, cuts):
+        def look_up(k, half_start, cuts, last_round=nc.scalar.copy):
             product = products.tile([P, HALF], F32, name="product")
             rounded = rounded_pool.tile([P, HALF], BF16, name="rounded")
             for start, size in cuts:
@@ -94,7 +94,8 @@ def tile_jointembeddingclassifier_kernel(tc, cw, x, ws, bs, offs, out):
                     e_all[:, half_start + start : half_start + start + size],
                     MULT,
                 )
-                nc.scalar.copy(rounded[:, start : start + size], product[:, start : start + size])
+                round_on = last_round if (start, size) == cuts[-1] else nc.scalar.copy
+                round_on(rounded[:, start : start + size], product[:, start : start + size])
             return rounded
 
         def add_up(logits, rounded, k, start, size):
@@ -106,9 +107,9 @@ def tile_jointembeddingclassifier_kernel(tc, cw, x, ws, bs, offs, out):
                 stop=(k == CHILDREN - 1),
             )
 
-        def store(logits, first_sample, size):
+        def store(logits, first_sample, size, copy_on=nc.scalar.copy):
             staged = staging.tile([CHILDREN, size], F32, name="staged")
-            nc.scalar.copy(staged[:], logits[:])
+            copy_on(staged[:], logits[:])
             nc.sync.dma_start(out[:, first_sample : first_sample + size], staged[:])
 
         first_logits = logit_banks.tile([CHILDREN, HALF], F32, name="first_logits")
@@ -119,8 +120,8 @@ def tile_jointembeddingclassifier_kernel(tc, cw, x, ws, bs, offs, out):
         def first_half(k, cuts):
             add_up(first_logits, look_up(k, 0, cuts), k, 0, HALF)
 
-        def second_half(k, cuts):
-            rounded = look_up(k, HALF, cuts)
+        def second_half(k, cuts, last_round=nc.scalar.copy):
+            rounded = look_up(k, HALF, cuts, last_round)
             for range_logits, (start, size) in zip(tail_logits, TAIL):
                 add_up(range_logits, rounded, k, start, size)
 
@@ -130,6 +131,8 @@ def tile_jointembeddingclassifier_kernel(tc, cw, x, ws, bs, offs, out):
             if group == GROUPS[-1]:
                 store(first_logits, 0, HALF)
             for k in group:
-                second_half(k, TAIL if k == CHILDREN - 1 else WHOLE)
-        for range_logits, (start, size) in zip(tail_logits, TAIL):
-            store(range_logits, HALF + start, size)
+                if k < CHILDREN - 1:
+                    second_half(k, WHOLE)
+        second_half(CHILDREN - 1, TAIL, last_round=nc.vector.tensor_copy)
+        store(tail_logits[0], HALF + TAIL[0][0], TAIL[0][1], copy_on=nc.scalar.copy)
+        store(tail_logits[1], HALF + TAIL[1][0], TAIL[1][1], copy_on=nc.vector.tensor_copy)

@@ -20,7 +20,7 @@ WHOLE = ((0, HALF),)
 BY_PARTS = ((0, PART), (PART, PART))
 SHORT = 256
 TAIL = ((0, HALF - SHORT), (HALF - SHORT, SHORT))
-GROUPS = ((0, 1), (2, 3), (4, 5, 6, 7))
+GROUPS = ((0, 1, 2, 3), (4, 5, 6, 7))
 assert all(start % (2 * LIST_COLUMN) == 0 for start, size in BY_PARTS + TAIL)
 
 FLOPS = 2 * D_IN * P * SAMPLES + 2 * CHILDREN * P * SAMPLES

@@ -32,7 +32,7 @@ def tile_jointembeddingclassifier_kernel(tc, cw, x, ws, bs, offs, out):
         tc.tile_pool(name="held", bufs=1) as held,
         tc.tile_pool(name="products", bufs=4) as products,
         tc.tile_pool(name="rounded", bufs=4) as rounded_pool,
-        tc.tile_pool(name="staging", bufs=2) as staging,
+        tc.tile_pool(name="staging", bufs=3) as staging,
         tc.psum_pool(name="e_banks", bufs=3) as e_banks,
         tc.psum_pool(name="logit_banks", bufs=1) as logit_banks,
     ):

import concourse.mybir as mybir

F32 = mybir.dt.float32
BF16 = mybir.dt.bfloat16
U16 = mybir.dt.uint16
MULT = mybir.AluOpType.mult
IDENTITY = mybir.ActivationFunctionType.Identity

P = 128
D_IN = 256
CHUNKS = D_IN // P
CHILDREN = 8
PARENTS = 512
SAMPLES = 1024
LIST_COLUMN = 16

HALF = PARENTS
PART = HALF // 2
WHOLE = ((0, HALF),)
BY_PARTS = ((0, PART), (PART, PART))
SHORT = 256
TAIL = ((0, HALF - SHORT), (HALF - SHORT, SHORT))
GROUPS = ((0, 1, 2, 3), (4, 5, 6, 7))
assert all(start % (2 * LIST_COLUMN) == 0 for start, size in BY_PARTS + TAIL)

FLOPS = 2 * D_IN * P * SAMPLES + 2 * CHILDREN * P * SAMPLES


def tile_jointembeddingclassifier_kernel(tc, cw, x, ws, bs, offs, out):
    nc = tc.nc
    with (
        tc.tile_pool(name="held", bufs=1) as held,
        tc.tile_pool(name="products", bufs=4) as products,
        tc.tile_pool(name="rounded", bufs=4) as rounded_pool,
        tc.tile_pool(name="staging", bufs=3) as staging,
        tc.psum_pool(name="e_banks", bufs=3) as e_banks,
        tc.psum_pool(name="logit_banks", bufs=1) as logit_banks,
    ):
        ws_chunks = held.tile([P, CHUNKS, P], BF16, name="ws_chunks")
        x_chunks = held.tile([P, CHUNKS, SAMPLES], BF16, name="x_chunks")
        x_by_chunk = x.rearrange("(p c) j -> p c j", c=CHUNKS)
        blocks = [held.tile([P, PARENTS], F32, name=f"block{k}") for k in range(CHILDREN)]
        bias = held.tile([P, 1], F32, name="bias")
        offsets = held.tile([P, SAMPLES // LIST_COLUMN], U16, name="offsets")

        def load_x(start, size):
            nc.sync.dma_start(x_chunks[:, :, start : start + size], x_by_chunk[:, :, start : start + size])

        def load_block(queue, k):
            queue.dma_start(blocks[k][:], cw[k * P : (k + 1) * P, :])

        nc.scalar.dma_start(ws_chunks[:], ws.rearrange("(p c) d -> p c d", c=CHUNKS))
        load_x(0, HALF)
        load_block(nc.sync, 0)
        nc.sync.dma_start(bias[:], bs)
        nc.sync.dma_start(offsets[:], offs)
        load_x(HALF, HALF)
        for k in range(1, CHILDREN):
            load_block(nc.sync, k)

        selector = held.tile([P, 2 * CHILDREN - 1], BF16, name="selector")
        nc.gpsimd.memset(selector[:], 0.0)
        nc.gpsimd.memset(selector[:, CHILDREN - 1 : CHILDREN], 1.0)

        cold = held.tile([P, 1], F32, name="cold")
        nc.gpsimd.memset(cold[:], 0.0)
        warm = held.tile([P, 1], F32, name="warm")
        nc.scalar.copy(warm[:], cold[:])

        e_all = held.tile([P, SAMPLES], F32, name="e_all")
        for start, size in BY_PARTS + ((HALF, HALF),):
            e_psum = e_banks.tile([P, size], F32, name="e_psum")
            for c in range(CHUNKS):
                nc.tensor.matmul(
                    e_psum[:],
                    ws_chunks[:, c, :],
                    x_chunks[:, c, start : start + size],
                    start=(c == 0),
                    stop=(c == CHUNKS - 1),
                )
            if start == 0:
                nc.vector.tensor_scalar_add(e_all[:, start : start + size], e_psum[:], bias[:])
            else:
                nc.scalar.activation(e_all[:, start : start + size], e_psum[:], IDENTITY, bias=bias[:])

        def look_up(k, half_start, cuts, last_round=nc.scalar.copy):
            product = products.tile([P, HALF], F32, name="product")
            rounded = rounded_pool.tile([P, HALF], BF16, name="rounded")
            for start, size in cuts:
                first_column = (half_start + start) // LIST_COLUMN
                nc.vector.tensor_tensor(
                    product[:, start : start + size],
                    blocks[k][:].indirect(offsets[:, first_column : first_column + size // LIST_COLUMN]),
                    e_all[:, half_start + start : half_start + start + size],
                    MULT,
                )
                round_on = last_round if (start, size) == cuts[-1] else nc.scalar.copy
                round_on(rounded[:, start : start + size], product[:, start : start + size])
            return rounded

        def add_up(logits, rounded, k, start, size):
            nc.tensor.matmul(
                logits[:],
                selector[:, CHILDREN - 1 - k : 2 * CHILDREN - 1 - k],
                rounded[:, start : start + size],
                start=(k == 0),
                stop=(k == CHILDREN - 1),
            )

        def store(logits, first_sample, size, copy_on=nc.scalar.copy):
            staged = staging.tile([CHILDREN, size], F32, name="staged")
            copy_on(staged[:], logits[:])
            nc.sync.dma_start(out[:, first_sample : first_sample + size], staged[:])

        first_logits = logit_banks.tile([CHILDREN, HALF], F32, name="first_logits")
        tail_logits = [
            logit_banks.tile([CHILDREN, size], F32, name=f"tail_logits{start}") for start, size in TAIL
        ]

        def first_half(k, cuts):
            add_up(first_logits, look_up(k, 0, cuts), k, 0, HALF)

        def second_half(k, cuts, last_round=nc.scalar.copy):
            rounded = look_up(k, HALF, cuts, last_round)
            for range_logits, (start, size) in zip(tail_logits, TAIL):
                add_up(range_logits, rounded, k, start, size)

        for group in GROUPS:
            for k in group:
                first_half(k, BY_PARTS if k == 0 else WHOLE)
            if group == GROUPS[-1]:
                store(first_logits, 0, HALF)
            for k in group:
                if k < CHILDREN - 1:
                    second_half(k, WHOLE)
        second_half(CHILDREN - 1, TAIL, last_round=nc.vector.tensor_copy)
        store(tail_logits[0], HALF + TAIL[0][0], TAIL[0][1], copy_on=nc.scalar.copy)
        store(tail_logits[1], HALF + TAIL[1][0], TAIL[1][1], copy_on=nc.vector.tensor_copy)
